import numpy as np
import ml_dtypes


def mxq(x, axis, fmt="e4m3"):
    dtype, down = {"e4m3": (ml_dtypes.float8_e4m3fn, 7), "e5m2": (ml_dtypes.float8_e5m2, 14)}[fmt]
    v = np.moveaxis(np.asarray(x, np.float32).astype(ml_dtypes.bfloat16).astype(np.float64), axis, -1)
    blocks = v.reshape(v.shape[:-1] + (-1, 32))
    amax = np.abs(blocks).max(-1, keepdims=True)
    byte = np.maximum(np.where(amax > 0, np.frexp(amax)[1] - 1 + 127, 0) - down, 1)
    scale = np.exp2(byte - 127.0)
    codes = (blocks / scale).astype(np.float32).astype(dtype).astype(np.float64)
    return np.moveaxis((codes * scale).reshape(v.shape), -1, axis)


WIDE = False


def mx_kscale(k):
    if not WIDE:
        return np.ones(k)
    levels = np.array([10, -10, 5, -5, 0])
    a = np.random.permutation(np.resize(levels, k // 512 * 4)).reshape(k // 512, 4)
    idx = np.arange(k)
    return np.exp2(a[idx // 512, idx % 128 // 32])


BF16 = ml_dtypes.bfloat16


def bf(x):
    return np.asarray(x, np.float32).astype(BF16)


def f64(x):
    return np.asarray(x).astype(np.float64)


B, C, H, W = 1, 512, 32, 32
N = H * W
SQ = np.sqrt(1.5 / np.sqrt(C))


def setup_inputs():
    s = mx_kscale(C)
    return {
        "c_feat": bf(np.random.standard_normal((B, C, N)) * SQ),
        "b_feat": bf(np.random.standard_normal((B, C, N)) * SQ),
        "x": bf(np.random.standard_normal((B, C, H, W)) * s[None, :, None, None]),
        "w3": bf(np.random.standard_normal((C, C)) * 2.0 / np.sqrt(C) * s[:, None] / s[None, :]),
        "b3": bf(np.random.standard_normal(C) * 0.3 * s),
        "alpha": bf(2.0 + 0.2 * np.random.standard_normal(1)),
    }


def reference(c_feat, b_feat, x, w3, b3, alpha):
    xf = f64(x).reshape(B, C, N)
    d_feat = (mxq(f64(w3), 1, "e4m3") @ mxq(xf, 1, "e4m3")) + f64(b3)[None, :, None]
    scores = f64(c_feat).transpose(0, 2, 1) @ f64(b_feat)
    p = np.exp(scores - scores.max(axis=1, keepdims=True))
    A = p / p.sum(axis=1, keepdims=True)
    attn = mxq(d_feat, 2, "e4m3") @ mxq(A, 2, "e4m3").transpose(0, 2, 1)
    return f64(x) + f64(alpha) * attn.reshape(B, C, H, W)

@@ -1,0 +1,217 @@
+from contextlib import ExitStack
+
+import concourse.mybir as mybir
+from concourse.masks import make_identity
+
+BF16 = mybir.dt.bfloat16
+F32 = mybir.dt.float32
+U32 = mybir.dt.uint32
+U8 = mybir.dt.uint8
+FP8X4 = mybir.dt.float8_e4m3fn_x4
+ALU = mybir.AluOpType
+ACT = mybir.ActivationFunctionType
+AX = mybir.AxisListType
+
+P = 128
+PACK = 4
+CHANNELS = 512
+PIXELS = 1024
+BANK = 512
+C_CHUNKS = CHANNELS // P
+J_PASSES = PIXELS // (P * PACK)
+HALVES = PIXELS // BANK
+RUN = 4
+
+FLOPS = 2 * CHANNELS * CHANNELS * PIXELS + 2 * 2 * PIXELS * PIXELS * CHANNELS
+
+
+def tile_dualattention_pa_kernel(tc, c_feat, b_feat, x, w3, b3, alpha, out):
+    nc = tc.nc
+    c_dram = c_feat.rearrange("b c n -> (b c) n")
+    b_dram = b_feat.rearrange("b c n -> (b c) n")
+    x_dram = x.rearrange("b c h w -> (b c) (h w)")
+    out_dram = out.rearrange("b c h w -> (b c) (h w)")
+
+    with ExitStack() as pools:
+        keep = pools.enter_context(tc.tile_pool(name="keep", bufs=1))
+        exp_pool = pools.enter_context(tc.tile_pool(name="exp", bufs=3))
+        res_pool = pools.enter_context(tc.tile_pool(name="res", bufs=4))
+        psum = pools.enter_context(tc.psum_pool(name="psum", bufs=8))
+
+        b_view = b_dram.rearrange("(cc p) j -> p cc j", p=P)
+        b_sb = [keep.tile([P, C_CHUNKS, BANK], BF16, name="b_sb%d" % g) for g in range(J_PASSES)]
+        c_sb = [keep.tile([P, PIXELS], BF16, name="c_sb%d" % cc) for cc in range(C_CHUNKS)]
+        nc.sync.dma_start(out=b_sb[0][:], in_=b_view[:, :, 0:BANK])
+        for cc in range(C_CHUNKS):
+            nc.sync.dma_start(out=c_sb[cc][:], in_=c_dram[cc * P : (cc + 1) * P, :])
+        nc.sync.dma_start(out=b_sb[1][:], in_=b_view[:, :, BANK : 2 * BANK])
+        x_sb = keep.tile([P, PACK, PIXELS], BF16, name="x_sb")
+        nc.sync.dma_start(out=x_sb[:], in_=x_dram.rearrange("(t p) j -> p t j", p=P))
+        w_sb = keep.tile([P, C_CHUNKS, CHANNELS], BF16, name="w_sb")
+        nc.sync.dma_start(out=w_sb[:], in_=w3.rearrange("(ot p) c -> p ot c", p=P))
+        bias_sb = keep.tile([P, CHANNELS], BF16, name="bias_sb")
+        nc.sync.dma_start(out=bias_sb[:], in_=b3.partition_broadcast(P))
+        alpha_bf = keep.tile([P, 1], BF16, name="alpha_bf")
+        nc.sync.dma_start(out=alpha_bf[:], in_=alpha.partition_broadcast(P))
+        alpha_f32 = keep.tile([P, 1], F32, name="alpha_f32")
+        nc.vector.tensor_copy(out=alpha_f32[:], in_=alpha_bf[:])
+
+        identity = keep.tile([P, P], BF16, name="identity")
+        make_identity(nc, identity[:])
+
+        x_grouped = keep.tile([P, PIXELS, PACK], BF16, name="x_grouped", align_bytes=64)
+        x_codes = keep.tile([P, PIXELS], U32, name="x_codes", align_bytes=64)
+        x_scales = keep.tile([P, PIXELS], U8, name="x_scales", align_bytes=64)
+        w_grouped = keep.tile([P, CHANNELS, PACK], BF16, name="w_grouped", align_bytes=64)
+        w_codes = keep.tile([P, CHANNELS], U32, name="w_codes", align_bytes=64)
+        w_scales = keep.tile([P, CHANNELS], U8, name="w_scales", align_bytes=64)
+        d_grouped = [
+            keep.tile([P, CHANNELS, PACK], BF16, name="d_grouped%d" % g, align_bytes=64) for g in range(J_PASSES)
+        ]
+        d_codes = [keep.tile([P, CHANNELS], U32, name="d_codes%d" % g, align_bytes=64) for g in range(J_PASSES)]
+        d_scales = [keep.tile([P, CHANNELS], U8, name="d_scales%d" % g, align_bytes=64) for g in range(J_PASSES)]
+        a_rows = [keep.tile([P, PACK, PIXELS], BF16, name="a_rows%d" % g) for g in range(J_PASSES)]
+        a_grouped = [
+            keep.tile([P, PIXELS, PACK], BF16, name="a_grouped%d" % g, align_bytes=64) for g in range(J_PASSES)
+        ]
+        a_codes = [keep.tile([P, PIXELS], U32, name="a_codes%d" % g, align_bytes=64) for g in range(J_PASSES)]
+        a_scales = [keep.tile([P, PIXELS], U8, name="a_scales%d" % g, align_bytes=64) for g in range(J_PASSES)]
+        j_tiles = J_PASSES * PACK
+        bank_max = keep.tile([P, j_tiles, HALVES], F32, name="bank_max")
+        neg_max = keep.tile([P, j_tiles], F32, name="neg_max")
+        bank_sum = keep.tile([P, j_tiles, HALVES], F32, name="bank_sum")
+        total = keep.tile([P, j_tiles], F32, name="total")
+        inv_total = keep.tile([P, j_tiles], F32, name="inv_total")
+
+        def regroup(grouped, rows, cols):
+            nc.vector.tensor_copy(
+                out=grouped[:, cols, :].rearrange("p (c i) t -> p c t i", i=RUN),
+                in_=rows[:, :, cols].rearrange("p t (c i) -> p c t i", i=RUN),
+            )
+
+        def quantise(codes, scales, grouped, cols):
+            nc.vector.quantize_mx(
+                out=codes[:, cols].bitcast(FP8X4),
+                scales=scales[:, cols],
+                in_=grouped[:, cols, :].rearrange("p col t -> p (col t)"),
+            )
+
+        def half(h):
+            return slice(h * BANK, (h + 1) * BANK)
+
+        def tile_of(index):
+            return slice(index * P, (index + 1) * P)
+
+        def softmax_tile(g, t):
+            jt = g * PACK + t
+            banks = [psum.tile([P, BANK], F32, name="score_bank", tag="bank") for h in range(HALVES)]
+            for cc in range(C_CHUNKS):
+                for h in range(HALVES):
+                    nc.tensor.matmul(
+                        out=banks[h][:],
+                        lhsT=b_sb[g][:, cc, tile_of(t)],
+                        rhs=c_sb[cc][:, half(h)],
+                        start=(cc == 0),
+                        stop=(cc == C_CHUNKS - 1),
+                    )
+            for h in range(HALVES):
+                nc.vector.tensor_reduce(out=bank_max[:, jt, h : h + 1], in_=banks[h][:], axis=AX.X, op=ALU.max)
+            nc.vector.tensor_reduce(
+                out=neg_max[:, jt : jt + 1], in_=bank_max[:, jt, :], axis=AX.X, op=ALU.max, negate=True
+            )
+            e = exp_pool.tile([P, PIXELS], F32, name="e")
+            for h in range(HALVES):
+                nc.scalar.activation(
+                    out=e[:, half(h)],
+                    in_=banks[h][:],
+                    func=ACT.Exp,
+                    bias=neg_max[:, jt : jt + 1],
+                    scale=1.0,
+                    accum_out=bank_sum[:, jt, h : h + 1],
+                )
+            nc.vector.tensor_reduce(out=total[:, jt : jt + 1], in_=bank_sum[:, jt, :], axis=AX.X, op=ALU.add)
+            nc.vector.reciprocal(out=inv_total[:, jt : jt + 1], in_=total[:, jt : jt + 1])
+            nc.scalar.activation(out=a_rows[g][:, t, :], in_=e[:], func=ACT.Copy, scale=inv_total[:, jt : jt + 1])
+
+        def quantise_a(g):
+            for h in range(HALVES):
+                regroup(a_grouped[g], a_rows[g], half(h))
+            for h in range(HALVES):
+                quantise(a_codes[g], a_scales[g], a_grouped[g], half(h))
+
+        def quantise_x_and_w3():
+            for h in range(HALVES):
+                regroup(x_grouped, x_sb, half(h))
+            for oh in range(2):
+                wt = psum.tile([P, PACK, 2 * P], BF16, name="wt", tag="bank")
+                for t in range(PACK):
+                    for o2 in range(2):
+                        nc.tensor.transpose(wt[:, t, tile_of(o2)], w_sb[:, 2 * oh + o2, tile_of(t)], identity[:])
+                nc.scalar.copy(
+                    out=w_grouped[:, oh * 2 * P : (oh + 1) * 2 * P, :], in_=wt[:].rearrange("p t o -> p o t")
+                )
+            for h in range(HALVES):
+                quantise(x_codes, x_scales, x_grouped, half(h))
+            quantise(w_codes, w_scales, w_grouped, slice(0, CHANNELS))
+
+        def project(g):
+            for oc in range(C_CHUNKS):
+                bank = psum.tile([P, PACK, P], F32, name="d_bank", tag="bank")
+                for t in range(PACK):
+                    nc.tensor.matmul_mx(
+                        out=bank[:, t, :],
+                        lhsT=x_codes[:, tile_of(g * PACK + t)].bitcast(FP8X4),
+                        lhsT_scale=x_scales[:, tile_of(g * PACK + t)],
+                        rhs=w_codes[:, tile_of(oc)].bitcast(FP8X4),
+                        rhs_scale=w_scales[:, tile_of(oc)],
+                        start=True,
+                        stop=True,
+                    )
+                nc.vector.tensor_tensor(
+                    out=d_grouped[g][:, tile_of(oc), :],
+                    in0=bank[:].rearrange("p t o -> p o t"),
+                    in1=bias_sb[:, tile_of(oc)].unsqueeze(2).to_broadcast([P, P, PACK]),
+                    op=ALU.add,
+                )
+            quantise(d_codes[g], d_scales[g], d_grouped[g], slice(0, CHANNELS))
+
+        softmax_tile(0, 0)
+        softmax_tile(0, 1)
+        quantise_x_and_w3()
+        softmax_tile(0, 2)
+        softmax_tile(0, 3)
+        project(0)
+        quantise_a(0)
+        softmax_tile(1, 0)
+        softmax_tile(1, 1)
+        project(1)
+        softmax_tile(1, 2)
+        softmax_tile(1, 3)
+        quantise_a(1)
+
+        blocks = [(h, ct) for h in range(HALVES) for ct in range(C_CHUNKS)]
+        acc = {}
+        for g in range(J_PASSES):
+            for h, ct in blocks:
+                if g == 0:
+                    acc[(h, ct)] = psum.tile([P, BANK], F32, name="acc", tag="bank")
+                nc.tensor.matmul_mx(
+                    out=acc[(h, ct)][:],
+                    lhsT=d_codes[g][:, tile_of(ct)].bitcast(FP8X4),
+                    lhsT_scale=d_scales[g][:, tile_of(ct)],
+                    rhs=a_codes[g][:, half(h)].bitcast(FP8X4),
+                    rhs_scale=a_scales[g][:, half(h)],
+                    start=(g == 0),
+                    stop=(g == J_PASSES - 1),
+                )
+        for h, ct in blocks:
+            res = res_pool.tile([P, BANK], F32, name="res")
+            nc.vector.scalar_tensor_tensor(
+                out=res[:],
+                in0=acc[(h, ct)][:],
+                scalar=alpha_f32[:, 0:1],
+                in1=x_sb[:, ct, half(h)],
+                op0=ALU.mult,
+                op1=ALU.add,
+            )
+            nc.sync.dma_start(out=out_dram[tile_of(ct), half(h)], in_=res[:])

@@ -34,9 +34,10 @@ def tile_dualattention_pa_kernel(tc, c_feat, b_feat, x, w3, b3, alpha, out):
 
     with ExitStack() as pools:
         keep = pools.enter_context(tc.tile_pool(name="keep", bufs=1))
-        exp_pool = pools.enter_context(tc.tile_pool(name="exp", bufs=3))
-        res_pool = pools.enter_context(tc.tile_pool(name="res", bufs=4))
+        exp_pool = pools.enter_context(tc.tile_pool(name="exp", bufs=4))
+        res_pool = pools.enter_context(tc.tile_pool(name="res", bufs=8))
         psum = pools.enter_context(tc.psum_pool(name="psum", bufs=8))
+        pools.enter_context(tc.manual_schedule())
 
         b_view = b_dram.rearrange("(cc p) j -> p cc j", p=P)
         b_sb = [keep.tile([P, C_CHUNKS, BANK], BF16, name="b_sb%d" % g) for g in range(J_PASSES)]
@@ -44,17 +45,16 @@ def tile_dualattention_pa_kernel(tc, c_feat, b_feat, x, w3, b3, alpha, out):
         nc.sync.dma_start(out=b_sb[0][:], in_=b_view[:, :, 0:BANK])
         for cc in range(C_CHUNKS):
             nc.sync.dma_start(out=c_sb[cc][:], in_=c_dram[cc * P : (cc + 1) * P, :])
-        nc.sync.dma_start(out=b_sb[1][:], in_=b_view[:, :, BANK : 2 * BANK])
         x_sb = keep.tile([P, PACK, PIXELS], BF16, name="x_sb")
         nc.sync.dma_start(out=x_sb[:], in_=x_dram.rearrange("(t p) j -> p t j", p=P))
         w_sb = keep.tile([P, C_CHUNKS, CHANNELS], BF16, name="w_sb")
         nc.sync.dma_start(out=w_sb[:], in_=w3.rearrange("(ot p) c -> p ot c", p=P))
+        nc.sync.dma_start(out=b_sb[1][:], in_=b_view[:, :, BANK : 2 * BANK])
         bias_sb = keep.tile([P, CHANNELS], BF16, name="bias_sb")
         nc.sync.dma_start(out=bias_sb[:], in_=b3.partition_broadcast(P))
         alpha_bf = keep.tile([P, 1], BF16, name="alpha_bf")
         nc.sync.dma_start(out=alpha_bf[:], in_=alpha.partition_broadcast(P))
         alpha_f32 = keep.tile([P, 1], F32, name="alpha_f32")
-        nc.vector.tensor_copy(out=alpha_f32[:], in_=alpha_bf[:])
 
         identity = keep.tile([P, P], BF16, name="identity")
         make_identity(nc, identity[:])
@@ -83,8 +83,17 @@ def tile_dualattention_pa_kernel(tc, c_feat, b_feat, x, w3, b3, alpha, out):
         total = keep.tile([P, j_tiles], F32, name="total")
         inv_total = keep.tile([P, j_tiles], F32, name="inv_total")
 
-        def regroup(grouped, rows, cols):
-            nc.vector.tensor_copy(
+        def half(h):
+            return slice(h * BANK, (h + 1) * BANK)
+
+        def quarter(q):
+            return slice(q * BANK // 2, (q + 1) * BANK // 2)
+
+        def tile_of(index):
+            return slice(index * P, (index + 1) * P)
+
+        def regroup(engine_copy, grouped, rows, cols):
+            engine_copy(
                 out=grouped[:, cols, :].rearrange("p (c i) t -> p c t i", i=RUN),
                 in_=rows[:, :, cols].rearrange("p t (c i) -> p c t i", i=RUN),
             )
@@ -96,52 +105,59 @@ def tile_dualattention_pa_kernel(tc, c_feat, b_feat, x, w3, b3, alpha, out):
                 in_=grouped[:, cols, :].rearrange("p col t -> p (col t)"),
             )
 
-        def half(h):
-            return slice(h * BANK, (h + 1) * BANK)
+        score_banks = {}
+        exps = {}
 
-        def tile_of(index):
-            return slice(index * P, (index + 1) * P)
-
-        def softmax_tile(g, t):
-            jt = g * PACK + t
-            banks = [psum.tile([P, BANK], F32, name="score_bank", tag="bank") for h in range(HALVES)]
+        def scores(jt):
+            g, t = divmod(jt, PACK)
+            score_banks[jt] = [psum.tile([P, BANK], F32, name="score_bank", tag="bank") for h in range(HALVES)]
             for cc in range(C_CHUNKS):
                 for h in range(HALVES):
                     nc.tensor.matmul(
-                        out=banks[h][:],
+                        out=score_banks[jt][h][:],
                         lhsT=b_sb[g][:, cc, tile_of(t)],
                         rhs=c_sb[cc][:, half(h)],
                         start=(cc == 0),
                         stop=(cc == C_CHUNKS - 1),
                     )
+
+        def maximum(jt):
             for h in range(HALVES):
-                nc.vector.tensor_reduce(out=bank_max[:, jt, h : h + 1], in_=banks[h][:], axis=AX.X, op=ALU.max)
+                nc.vector.tensor_reduce(
+                    out=bank_max[:, jt, h : h + 1], in_=score_banks[jt][h][:], axis=AX.X, op=ALU.max
+                )
             nc.vector.tensor_reduce(
                 out=neg_max[:, jt : jt + 1], in_=bank_max[:, jt, :], axis=AX.X, op=ALU.max, negate=True
             )
-            e = exp_pool.tile([P, PIXELS], F32, name="e")
+
+        def exponentials(jt):
+            exps[jt] = exp_pool.tile([P, PIXELS], F32, name="e")
             for h in range(HALVES):
                 nc.scalar.activation(
-                    out=e[:, half(h)],
-                    in_=banks[h][:],
+                    out=exps[jt][:, half(h)],
+                    in_=score_banks[jt][h][:],
                     func=ACT.Exp,
                     bias=neg_max[:, jt : jt + 1],
                     scale=1.0,
                     accum_out=bank_sum[:, jt, h : h + 1],
                 )
+
+        def inverse_total(jt):
             nc.vector.tensor_reduce(out=total[:, jt : jt + 1], in_=bank_sum[:, jt, :], axis=AX.X, op=ALU.add)
             nc.vector.reciprocal(out=inv_total[:, jt : jt + 1], in_=total[:, jt : jt + 1])
-            nc.scalar.activation(out=a_rows[g][:, t, :], in_=e[:], func=ACT.Copy, scale=inv_total[:, jt : jt + 1])
 
-        def quantise_a(g):
-            for h in range(HALVES):
-                regroup(a_grouped[g], a_rows[g], half(h))
-            for h in range(HALVES):
-                quantise(a_codes[g], a_scales[g], a_grouped[g], half(h))
+        def normalise(jt):
+            g, t = divmod(jt, PACK)
+            nc.gpsimd.tensor_scalar(
+                out=a_rows[g][:, t, :],
+                in0=exps[jt][:],
+                scalar1=inv_total[:, jt : jt + 1],
+                scalar2=0.0,
+                op0=ALU.mult,
+                op1=ALU.add,
+            )
 
-        def quantise_x_and_w3():
-            for h in range(HALVES):
-                regroup(x_grouped, x_sb, half(h))
+        def transpose_w3():
             for oh in range(2):
                 wt = psum.tile([P, PACK, 2 * P], BF16, name="wt", tag="bank")
                 for t in range(PACK):
@@ -150,16 +166,15 @@ def tile_dualattention_pa_kernel(tc, c_feat, b_feat, x, w3, b3, alpha, out):
                 nc.scalar.copy(
                     out=w_grouped[:, oh * 2 * P : (oh + 1) * 2 * P, :], in_=wt[:].rearrange("p t o -> p o t")
                 )
-            for h in range(HALVES):
-                quantise(x_codes, x_scales, x_grouped, half(h))
-            quantise(w_codes, w_scales, w_grouped, slice(0, CHANNELS))
+
+        d_banks = {}
 
         def project(g):
             for oc in range(C_CHUNKS):
-                bank = psum.tile([P, PACK, P], F32, name="d_bank", tag="bank")
+                d_banks[(g, oc)] = psum.tile([P, PACK, P], F32, name="d_bank", tag="bank")
                 for t in range(PACK):
                     nc.tensor.matmul_mx(
-                        out=bank[:, t, :],
+                        out=d_banks[(g, oc)][:, t, :],
                         lhsT=x_codes[:, tile_of(g * PACK + t)].bitcast(FP8X4),
                         lhsT_scale=x_scales[:, tile_of(g * PACK + t)],
                         rhs=w_codes[:, tile_of(oc)].bitcast(FP8X4),
@@ -167,32 +182,19 @@ def tile_dualattention_pa_kernel(tc, c_feat, b_feat, x, w3, b3, alpha, out):
                         start=True,
                         stop=True,
                     )
-                nc.vector.tensor_tensor(
-                    out=d_grouped[g][:, tile_of(oc), :],
-                    in0=bank[:].rearrange("p t o -> p o t"),
-                    in1=bias_sb[:, tile_of(oc)].unsqueeze(2).to_broadcast([P, P, PACK]),
-                    op=ALU.add,
-                )
-            quantise(d_codes[g], d_scales[g], d_grouped[g], slice(0, CHANNELS))
 
-        softmax_tile(0, 0)
-        softmax_tile(0, 1)
-        quantise_x_and_w3()
-        softmax_tile(0, 2)
-        softmax_tile(0, 3)
-        project(0)
-        quantise_a(0)
-        softmax_tile(1, 0)
-        softmax_tile(1, 1)
-        project(1)
-        softmax_tile(1, 2)
-        softmax_tile(1, 3)
-        quantise_a(1)
+        def add_bias(g, oc):
+            nc.vector.tensor_tensor(
+                out=d_grouped[g][:, tile_of(oc), :],
+                in0=d_banks[(g, oc)][:].rearrange("p t o -> p o t"),
+                in1=bias_sb[:, tile_of(oc)].unsqueeze(2).to_broadcast([P, P, PACK]),
+                op=ALU.add,
+            )
 
-        blocks = [(h, ct) for h in range(HALVES) for ct in range(C_CHUNKS)]
         acc = {}
-        for g in range(J_PASSES):
-            for h, ct in blocks:
+
+        def attend(g, h):
+            for ct in range(C_CHUNKS):
                 if g == 0:
                     acc[(h, ct)] = psum.tile([P, BANK], F32, name="acc", tag="bank")
                 nc.tensor.matmul_mx(
@@ -204,7 +206,8 @@ def tile_dualattention_pa_kernel(tc, c_feat, b_feat, x, w3, b3, alpha, out):
                     start=(g == 0),
                     stop=(g == J_PASSES - 1),
                 )
-        for h, ct in blocks:
+
+        def finish(h, ct):
             res = res_pool.tile([P, BANK], F32, name="res")
             nc.vector.scalar_tensor_tensor(
                 out=res[:],
@@ -215,3 +218,104 @@ def tile_dualattention_pa_kernel(tc, c_feat, b_feat, x, w3, b3, alpha, out):
                 op1=ALU.add,
             )
             nc.sync.dma_start(out=out_dram[tile_of(ct), half(h)], in_=res[:])
+
+        def normalise_on_vector(jt):
+            g, t = divmod(jt, PACK)
+            nc.vector.tensor_scalar(
+                out=a_rows[g][:, t, :], in0=exps[jt][:], scalar1=inv_total[:, jt : jt + 1], scalar2=None, op0=ALU.mult
+            )
+
+        def finish_by_two(h, ct):
+            scaled = res_pool.tile([P, BANK], F32, name="scaled")
+            nc.scalar.activation(out=scaled[:], in_=acc[(h, ct)][:], func=ACT.Copy, scale=alpha_f32[:, 0:1])
+            res = res_pool.tile([P, BANK], F32, name="res")
+            nc.gpsimd.tensor_tensor(out=res[:], in0=scaled[:], in1=x_sb[:, ct, half(h)], op=ALU.add)
+            nc.scalar.dma_start(out=out_dram[tile_of(ct), half(h)], in_=res[:])
+
+        all_channels = slice(0, CHANNELS)
+
+        scores(0)
+        maximum(0)
+        exponentials(0)
+
+        scores(1)
+        maximum(1)
+        exponentials(1)
+        regroup(nc.vector.tensor_copy, x_grouped, x_sb, half(0))
+        inverse_total(0)
+        normalise(0)
+
+        scores(2)
+        transpose_w3()
+        maximum(2)
+        exponentials(2)
+        regroup(nc.vector.tensor_copy, x_grouped, x_sb, half(1))
+        inverse_total(1)
+        normalise(1)
+
+        scores(3)
+        maximum(3)
+        exponentials(3)
+        quantise(x_codes, x_scales, x_grouped, half(0))
+        quantise(x_codes, x_scales, x_grouped, half(1))
+        inverse_total(2)
+        normalise(2)
+
+        scores(4)
+        maximum(4)
+        exponentials(4)
+        quantise(w_codes, w_scales, w_grouped, all_channels)
+        nc.vector.tensor_copy(out=alpha_f32[:], in_=alpha_bf[:])
+        inverse_total(3)
+        normalise(3)
+
+        scores(5)
+        project(0)
+        maximum(5)
+        exponentials(5)
+        regroup(nc.scalar.copy, a_grouped[0], a_rows[0], quarter(0))
+        for oc in range(C_CHUNKS):
+            add_bias(0, oc)
+        regroup(nc.scalar.copy, a_grouped[0], a_rows[0], quarter(1))
+        inverse_total(4)
+        normalise(4)
+
+        scores(6)
+        project(1)
+        maximum(6)
+        exponentials(6)
+        regroup(nc.scalar.copy, a_grouped[0], a_rows[0], quarter(2))
+        quantise(d_codes[0], d_scales[0], d_grouped[0], all_channels)
+        quantise(a_codes[0], a_scales[0], a_grouped[0], half(0))
+        add_bias(1, 0)
+        add_bias(1, 1)
+        regroup(nc.scalar.copy, a_grouped[0], a_rows[0], quarter(3))
+        inverse_total(5)
+        normalise(5)
+
+        scores(7)
+        attend(0, 0)
+        maximum(7)
+        exponentials(7)
+        add_bias(1, 2)
+        add_bias(1, 3)
+        quantise(a_codes[0], a_scales[0], a_grouped[0], half(1))
+        quantise(d_codes[1], d_scales[1], d_grouped[1], all_channels)
+        inverse_total(6)
+        normalise(6)
+        attend(0, 1)
+
+        inverse_total(7)
+        normalise_on_vector(7)
+        regroup(nc.scalar.copy, a_grouped[1], a_rows[1], half(1))
+        regroup(nc.vector.tensor_copy, a_grouped[1], a_rows[1], half(0))
+        quantise(a_codes[1], a_scales[1], a_grouped[1], half(0))
+        attend(1, 0)
+        quantise(a_codes[1], a_scales[1], a_grouped[1], half(1))
+        attend(1, 1)
+        for h in range(HALVES):
+            for ct in range(C_CHUNKS):
+                if ct == 1:
+                    finish_by_two(h, ct)
+                else:
+                    finish(h, ct)

@@ -121,11 +121,13 @@ def tile_dualattention_pa_kernel(tc, c_feat, b_feat, x, w3, b3, alpha, out):
                         stop=(cc == C_CHUNKS - 1),
                     )
 
-        def maximum(jt):
+        def bank_maxima(jt):
             for h in range(HALVES):
                 nc.vector.tensor_reduce(
                     out=bank_max[:, jt, h : h + 1], in_=score_banks[jt][h][:], axis=AX.X, op=ALU.max
                 )
+
+        def negated_maximum(jt):
             nc.vector.tensor_reduce(
                 out=neg_max[:, jt : jt + 1], in_=bank_max[:, jt, :], axis=AX.X, op=ALU.max, negate=True
             )
@@ -142,8 +144,10 @@ def tile_dualattention_pa_kernel(tc, c_feat, b_feat, x, w3, b3, alpha, out):
                     accum_out=bank_sum[:, jt, h : h + 1],
                 )
 
-        def inverse_total(jt):
+        def sum_of(jt):
             nc.vector.tensor_reduce(out=total[:, jt : jt + 1], in_=bank_sum[:, jt, :], axis=AX.X, op=ALU.add)
+
+        def reciprocal_of(jt):
             nc.vector.reciprocal(out=inv_total[:, jt : jt + 1], in_=total[:, jt : jt + 1])
 
         def normalise(jt):
@@ -235,77 +239,95 @@ def tile_dualattention_pa_kernel(tc, c_feat, b_feat, x, w3, b3, alpha, out):
         all_channels = slice(0, CHANNELS)
 
         scores(0)
-        maximum(0)
+        bank_maxima(0)
+        negated_maximum(0)
         exponentials(0)
 
         scores(1)
-        maximum(1)
+        bank_maxima(1)
+        sum_of(0)
+        negated_maximum(1)
         exponentials(1)
         regroup(nc.vector.tensor_copy, x_grouped, x_sb, half(0))
-        inverse_total(0)
+        reciprocal_of(0)
         normalise(0)
 
         scores(2)
         transpose_w3()
-        maximum(2)
+        bank_maxima(2)
+        sum_of(1)
+        negated_maximum(2)
         exponentials(2)
         regroup(nc.vector.tensor_copy, x_grouped, x_sb, half(1))
-        inverse_total(1)
+        reciprocal_of(1)
         normalise(1)
 
         scores(3)
-        maximum(3)
-        exponentials(3)
+        bank_maxima(3)
+        sum_of(2)
         quantise(x_codes, x_scales, x_grouped, half(0))
+        negated_maximum(3)
+        exponentials(3)
         quantise(x_codes, x_scales, x_grouped, half(1))
-        inverse_total(2)
+        reciprocal_of(2)
         normalise(2)
 
         scores(4)
-        maximum(4)
-        exponentials(4)
+        bank_maxima(4)
+        sum_of(3)
         quantise(w_codes, w_scales, w_grouped, all_channels)
+        negated_maximum(4)
+        exponentials(4)
         nc.vector.tensor_copy(out=alpha_f32[:], in_=alpha_bf[:])
-        inverse_total(3)
+        reciprocal_of(3)
         normalise(3)
 
         scores(5)
         project(0)
-        maximum(5)
+        bank_maxima(5)
+        sum_of(4)
+        add_bias(0, 0)
+        negated_maximum(5)
         exponentials(5)
         regroup(nc.scalar.copy, a_grouped[0], a_rows[0], quarter(0))
-        for oc in range(C_CHUNKS):
-            add_bias(0, oc)
+        add_bias(0, 1)
+        add_bias(0, 2)
+        add_bias(0, 3)
         regroup(nc.scalar.copy, a_grouped[0], a_rows[0], quarter(1))
-        inverse_total(4)
+        reciprocal_of(4)
         normalise(4)
 
         scores(6)
         project(1)
-        maximum(6)
+        bank_maxima(6)
+        sum_of(5)
+        quantise(d_codes[0], d_scales[0], d_grouped[0], all_channels)
+        negated_maximum(6)
         exponentials(6)
         regroup(nc.scalar.copy, a_grouped[0], a_rows[0], quarter(2))
-        quantise(d_codes[0], d_scales[0], d_grouped[0], all_channels)
         quantise(a_codes[0], a_scales[0], a_grouped[0], half(0))
         add_bias(1, 0)
         add_bias(1, 1)
         regroup(nc.scalar.copy, a_grouped[0], a_rows[0], quarter(3))
-        inverse_total(5)
+        reciprocal_of(5)
         normalise(5)
 
         scores(7)
         attend(0, 0)
-        maximum(7)
-        exponentials(7)
+        bank_maxima(7)
+        sum_of(6)
         add_bias(1, 2)
+        negated_maximum(7)
+        exponentials(7)
+        reciprocal_of(6)
+        normalise(6)
         add_bias(1, 3)
         quantise(a_codes[0], a_scales[0], a_grouped[0], half(1))
         quantise(d_codes[1], d_scales[1], d_grouped[1], all_channels)
-        inverse_total(6)
-        normalise(6)
         attend(0, 1)
 
-        inverse_total(7)
+        sum_of(7)
+        reciprocal_of(7)
         normalise_on_vector(7)
         regroup(nc.scalar.copy, a_grouped[1], a_rows[1], half(1))
         regroup(nc.vector.tensor_copy, a_grouped[1], a_rows[1], half(0))
@@ -315,7 +337,7 @@ def tile_dualattention_pa_kernel(tc, c_feat, b_feat, x, w3, b3, alpha, out):
         attend(1, 1)
         for h in range(HALVES):
             for ct in range(C_CHUNKS):
-                if ct == 1:
+                if h == 0 and ct % 2 == 1:
                     finish_by_two(h, ct)
                 else:
                     finish(h, ct)

@@ -229,13 +229,6 @@ def tile_dualattention_pa_kernel(tc, c_feat, b_feat, x, w3, b3, alpha, out):
                 out=a_rows[g][:, t, :], in0=exps[jt][:], scalar1=inv_total[:, jt : jt + 1], scalar2=None, op0=ALU.mult
             )
 
-        def finish_by_two(h, ct):
-            scaled = res_pool.tile([P, BANK], F32, name="scaled")
-            nc.scalar.activation(out=scaled[:], in_=acc[(h, ct)][:], func=ACT.Copy, scale=alpha_f32[:, 0:1])
-            res = res_pool.tile([P, BANK], F32, name="res")
-            nc.gpsimd.tensor_tensor(out=res[:], in0=scaled[:], in1=x_sb[:, ct, half(h)], op=ALU.add)
-            nc.scalar.dma_start(out=out_dram[tile_of(ct), half(h)], in_=res[:])
-
         all_channels = slice(0, CHANNELS)
 
         scores(0)
@@ -308,7 +301,6 @@ def tile_dualattention_pa_kernel(tc, c_feat, b_feat, x, w3, b3, alpha, out):
         quantise(a_codes[0], a_scales[0], a_grouped[0], half(0))
         add_bias(1, 0)
         add_bias(1, 1)
-        regroup(nc.scalar.copy, a_grouped[0], a_rows[0], quarter(3))
         reciprocal_of(5)
         normalise(5)
 
@@ -316,15 +308,14 @@ def tile_dualattention_pa_kernel(tc, c_feat, b_feat, x, w3, b3, alpha, out):
         attend(0, 0)
         bank_maxima(7)
         sum_of(6)
-        add_bias(1, 2)
         negated_maximum(7)
         exponentials(7)
+        regroup(nc.scalar.copy, a_grouped[0], a_rows[0], quarter(3))
         reciprocal_of(6)
         normalise(6)
+        add_bias(1, 2)
         add_bias(1, 3)
-        quantise(a_codes[0], a_scales[0], a_grouped[0], half(1))
         quantise(d_codes[1], d_scales[1], d_grouped[1], all_channels)
-        attend(0, 1)
 
         sum_of(7)
         reciprocal_of(7)
@@ -333,11 +324,10 @@ def tile_dualattention_pa_kernel(tc, c_feat, b_feat, x, w3, b3, alpha, out):
         regroup(nc.vector.tensor_copy, a_grouped[1], a_rows[1], half(0))
         quantise(a_codes[1], a_scales[1], a_grouped[1], half(0))
         attend(1, 0)
+        quantise(a_codes[0], a_scales[0], a_grouped[0], half(1))
+        attend(0, 1)
         quantise(a_codes[1], a_scales[1], a_grouped[1], half(1))
         attend(1, 1)
         for h in range(HALVES):
             for ct in range(C_CHUNKS):
-                if h == 0 and ct % 2 == 1:
-                    finish_by_two(h, ct)
-                else:
-                    finish(h, ct)
+                finish(h, ct)

@@ -20,6 +20,7 @@ BANK = 512
 C_CHUNKS = CHANNELS // P
 J_PASSES = PIXELS // (P * PACK)
 HALVES = PIXELS // BANK
+B_QUARTERS = 4
 RUN = 4
 
 FLOPS = 2 * CHANNELS * CHANNELS * PIXELS + 2 * 2 * PIXELS * PIXELS * CHANNELS
@@ -40,16 +41,22 @@ def tile_dualattention_pa_kernel(tc, c_feat, b_feat, x, w3, b3, alpha, out):
         pools.enter_context(tc.manual_schedule())
 
         b_view = b_dram.rearrange("(cc p) j -> p cc j", p=P)
-        b_sb = [keep.tile([P, C_CHUNKS, BANK], BF16, name="b_sb%d" % g) for g in range(J_PASSES)]
+        b_sb = [keep.tile([P, C_CHUNKS, 2 * P], BF16, name="b_sb%d" % q) for q in range(B_QUARTERS)]
         c_sb = [keep.tile([P, PIXELS], BF16, name="c_sb%d" % cc) for cc in range(C_CHUNKS)]
-        nc.sync.dma_start(out=b_sb[0][:], in_=b_view[:, :, 0:BANK])
+
+        def load_b(q):
+            nc.sync.dma_start(out=b_sb[q][:], in_=b_view[:, :, q * 2 * P : (q + 1) * 2 * P])
+
+        load_b(0)
         for cc in range(C_CHUNKS):
             nc.sync.dma_start(out=c_sb[cc][:], in_=c_dram[cc * P : (cc + 1) * P, :])
+        load_b(1)
         x_sb = keep.tile([P, PACK, PIXELS], BF16, name="x_sb")
         nc.sync.dma_start(out=x_sb[:], in_=x_dram.rearrange("(t p) j -> p t j", p=P))
         w_sb = keep.tile([P, C_CHUNKS, CHANNELS], BF16, name="w_sb")
         nc.sync.dma_start(out=w_sb[:], in_=w3.rearrange("(ot p) c -> p ot c", p=P))
-        nc.sync.dma_start(out=b_sb[1][:], in_=b_view[:, :, BANK : 2 * BANK])
+        load_b(2)
+        load_b(3)
         bias_sb = keep.tile([P, CHANNELS], BF16, name="bias_sb")
         nc.sync.dma_start(out=bias_sb[:], in_=b3.partition_broadcast(P))
         alpha_bf = keep.tile([P, 1], BF16, name="alpha_bf")
@@ -80,6 +87,7 @@ def tile_dualattention_pa_kernel(tc, c_feat, b_feat, x, w3, b3, alpha, out):
         bank_max = keep.tile([P, j_tiles, HALVES], F32, name="bank_max")
         neg_max = keep.tile([P, j_tiles], F32, name="neg_max")
         bank_sum = keep.tile([P, j_tiles, HALVES], F32, name="bank_sum")
+        sum_copy = keep.tile([P, j_tiles, HALVES], F32, name="sum_copy")
         total = keep.tile([P, j_tiles], F32, name="total")
         inv_total = keep.tile([P, j_tiles], F32, name="inv_total")
 
@@ -109,13 +117,12 @@ def tile_dualattention_pa_kernel(tc, c_feat, b_feat, x, w3, b3, alpha, out):
         exps = {}
 
         def scores(jt):
-            g, t = divmod(jt, PACK)
             score_banks[jt] = [psum.tile([P, BANK], F32, name="score_bank", tag="bank") for h in range(HALVES)]
             for cc in range(C_CHUNKS):
                 for h in range(HALVES):
                     nc.tensor.matmul(
                         out=score_banks[jt][h][:],
-                        lhsT=b_sb[g][:, cc, tile_of(t)],
+                        lhsT=b_sb[jt // 2][:, cc, tile_of(jt % 2)],
                         rhs=c_sb[cc][:, half(h)],
                         start=(cc == 0),
                         stop=(cc == C_CHUNKS - 1),
@@ -145,7 +152,9 @@ def tile_dualattention_pa_kernel(tc, c_feat, b_feat, x, w3, b3, alpha, out):
                 )
 
         def sum_of(jt):
-            nc.vector.tensor_reduce(out=total[:, jt : jt + 1], in_=bank_sum[:, jt, :], axis=AX.X, op=ALU.add)
+            nc.scalar.activation(
+                out=sum_copy[:, jt, :], in_=bank_sum[:, jt, :], func=ACT.Copy, accum_out=total[:, jt : jt + 1]
+            )
 
         def reciprocal_of(jt):
             nc.vector.reciprocal(out=inv_total[:, jt : jt + 1], in_=total[:, jt : jt + 1])
@@ -229,18 +238,30 @@ def tile_dualattention_pa_kernel(tc, c_feat, b_feat, x, w3, b3, alpha, out):
                 out=a_rows[g][:, t, :], in0=exps[jt][:], scalar1=inv_total[:, jt : jt + 1], scalar2=None, op0=ALU.mult
             )
 
+        scaled = {}
+
+        def scale_on_scalar(h, ct):
+            scaled[(h, ct)] = res_pool.tile([P, BANK], F32, name="scaled")
+            nc.scalar.activation(out=scaled[(h, ct)][:], in_=acc[(h, ct)][:], func=ACT.Copy, scale=alpha_f32[:, 0:1])
+
+        def add_x_on_gpsimd(h, ct):
+            res = res_pool.tile([P, BANK], F32, name="res")
+            nc.gpsimd.tensor_tensor(out=res[:], in0=scaled[(h, ct)][:], in1=x_sb[:, ct, half(h)], op=ALU.add)
+            nc.sync.dma_start(out=out_dram[tile_of(ct), half(h)], in_=res[:])
+
         all_channels = slice(0, CHANNELS)
 
         scores(0)
         bank_maxima(0)
         negated_maximum(0)
         exponentials(0)
+        sum_of(0)
 
         scores(1)
         bank_maxima(1)
-        sum_of(0)
         negated_maximum(1)
         exponentials(1)
+        sum_of(1)
         regroup(nc.vector.tensor_copy, x_grouped, x_sb, half(0))
         reciprocal_of(0)
         normalise(0)
@@ -248,29 +269,29 @@ def tile_dualattention_pa_kernel(tc, c_feat, b_feat, x, w3, b3, alpha, out):
         scores(2)
         transpose_w3()
         bank_maxima(2)
-        sum_of(1)
         negated_maximum(2)
         exponentials(2)
+        sum_of(2)
         regroup(nc.vector.tensor_copy, x_grouped, x_sb, half(1))
         reciprocal_of(1)
         normalise(1)
 
         scores(3)
         bank_maxima(3)
-        sum_of(2)
         quantise(x_codes, x_scales, x_grouped, half(0))
         negated_maximum(3)
         exponentials(3)
+        sum_of(3)
         quantise(x_codes, x_scales, x_grouped, half(1))
         reciprocal_of(2)
         normalise(2)
 
         scores(4)
         bank_maxima(4)
-        sum_of(3)
         quantise(w_codes, w_scales, w_grouped, all_channels)
         negated_maximum(4)
         exponentials(4)
+        sum_of(4)
         nc.vector.tensor_copy(out=alpha_f32[:], in_=alpha_bf[:])
         reciprocal_of(3)
         normalise(3)
@@ -278,10 +299,10 @@ def tile_dualattention_pa_kernel(tc, c_feat, b_feat, x, w3, b3, alpha, out):
         scores(5)
         project(0)
         bank_maxima(5)
-        sum_of(4)
         add_bias(0, 0)
         negated_maximum(5)
         exponentials(5)
+        sum_of(5)
         regroup(nc.scalar.copy, a_grouped[0], a_rows[0], quarter(0))
         add_bias(0, 1)
         add_bias(0, 2)
@@ -293,31 +314,30 @@ def tile_dualattention_pa_kernel(tc, c_feat, b_feat, x, w3, b3, alpha, out):
         scores(6)
         project(1)
         bank_maxima(6)
-        sum_of(5)
         quantise(d_codes[0], d_scales[0], d_grouped[0], all_channels)
         negated_maximum(6)
         exponentials(6)
+        sum_of(6)
         regroup(nc.scalar.copy, a_grouped[0], a_rows[0], quarter(2))
         quantise(a_codes[0], a_scales[0], a_grouped[0], half(0))
         add_bias(1, 0)
         add_bias(1, 1)
+        regroup(nc.scalar.copy, a_grouped[0], a_rows[0], quarter(3))
         reciprocal_of(5)
         normalise(5)
 
         scores(7)
         attend(0, 0)
         bank_maxima(7)
-        sum_of(6)
-        negated_maximum(7)
-        exponentials(7)
-        regroup(nc.scalar.copy, a_grouped[0], a_rows[0], quarter(3))
         reciprocal_of(6)
         normalise(6)
+        negated_maximum(7)
+        exponentials(7)
+        sum_of(7)
         add_bias(1, 2)
         add_bias(1, 3)
         quantise(d_codes[1], d_scales[1], d_grouped[1], all_channels)
 
-        sum_of(7)
         reciprocal_of(7)
         normalise_on_vector(7)
         regroup(nc.scalar.copy, a_grouped[1], a_rows[1], half(1))
@@ -328,6 +348,13 @@ def tile_dualattention_pa_kernel(tc, c_feat, b_feat, x, w3, b3, alpha, out):
         attend(0, 1)
         quantise(a_codes[1], a_scales[1], a_grouped[1], half(1))
         attend(1, 1)
-        for h in range(HALVES):
-            for ct in range(C_CHUNKS):
-                finish(h, ct)
+        scale_on_scalar(0, 1)
+        scale_on_scalar(0, 3)
+        finish(0, 0)
+        finish(0, 2)
+        add_x_on_gpsimd(0, 1)
+        finish(1, 0)
+        finish(1, 1)
+        add_x_on_gpsimd(0, 3)
+        finish(1, 2)
+        finish(1, 3)

@@ -259,20 +259,20 @@ def tile_dualattention_pa_kernel(tc, c_feat, b_feat, x, w3, b3, alpha, out):
 
         scores(1)
         bank_maxima(1)
+        regroup(nc.vector.tensor_copy, x_grouped, x_sb, half(0))
         negated_maximum(1)
         exponentials(1)
         sum_of(1)
-        regroup(nc.vector.tensor_copy, x_grouped, x_sb, half(0))
         reciprocal_of(0)
         normalise(0)
 
         scores(2)
         transpose_w3()
         bank_maxima(2)
+        regroup(nc.vector.tensor_copy, x_grouped, x_sb, half(1))
         negated_maximum(2)
         exponentials(2)
         sum_of(2)
-        regroup(nc.vector.tensor_copy, x_grouped, x_sb, half(1))
         reciprocal_of(1)
         normalise(1)
 
@@ -314,14 +314,14 @@ def tile_dualattention_pa_kernel(tc, c_feat, b_feat, x, w3, b3, alpha, out):
         scores(6)
         project(1)
         bank_maxima(6)
-        quantise(d_codes[0], d_scales[0], d_grouped[0], all_channels)
+        add_bias(1, 0)
         negated_maximum(6)
         exponentials(6)
         sum_of(6)
         regroup(nc.scalar.copy, a_grouped[0], a_rows[0], quarter(2))
-        quantise(a_codes[0], a_scales[0], a_grouped[0], half(0))
-        add_bias(1, 0)
         add_bias(1, 1)
+        quantise(d_codes[0], d_scales[0], d_grouped[0], all_channels)
+        quantise(a_codes[0], a_scales[0], a_grouped[0], half(0))
         regroup(nc.scalar.copy, a_grouped[0], a_rows[0], quarter(3))
         reciprocal_of(5)
         normalise(5)
@@ -337,6 +337,8 @@ def tile_dualattention_pa_kernel(tc, c_feat, b_feat, x, w3, b3, alpha, out):
         add_bias(1, 2)
         add_bias(1, 3)
         quantise(d_codes[1], d_scales[1], d_grouped[1], all_channels)
+        quantise(a_codes[0], a_scales[0], a_grouped[0], half(1))
+        attend(0, 1)
 
         reciprocal_of(7)
         normalise_on_vector(7)
@@ -344,8 +346,6 @@ def tile_dualattention_pa_kernel(tc, c_feat, b_feat, x, w3, b3, alpha, out):
         regroup(nc.vector.tensor_copy, a_grouped[1], a_rows[1], half(0))
         quantise(a_codes[1], a_scales[1], a_grouped[1], half(0))
         attend(1, 0)
-        quantise(a_codes[0], a_scales[0], a_grouped[0], half(1))
-        attend(0, 1)
         quantise(a_codes[1], a_scales[1], a_grouped[1], half(1))
         attend(1, 1)
         scale_on_scalar(0, 1)

@@ -21,6 +21,7 @@ C_CHUNKS = CHANNELS // P
 J_PASSES = PIXELS // (P * PACK)
 HALVES = PIXELS // BANK
 B_QUARTERS = 4
+WARM_UP = 4
 RUN = 4
 
 FLOPS = 2 * CHANNELS * CHANNELS * PIXELS + 2 * 2 * PIXELS * PIXELS * CHANNELS
@@ -48,8 +49,10 @@ def tile_dualattention_pa_kernel(tc, c_feat, b_feat, x, w3, b3, alpha, out):
             nc.sync.dma_start(out=b_sb[q][:], in_=b_view[:, :, q * 2 * P : (q + 1) * 2 * P])
 
         load_b(0)
-        for cc in range(C_CHUNKS):
-            nc.sync.dma_start(out=c_sb[cc][:], in_=c_dram[cc * P : (cc + 1) * P, :])
+        for h in range(HALVES):
+            for cc in range(C_CHUNKS):
+                cols = slice(h * BANK, (h + 1) * BANK)
+                nc.sync.dma_start(out=c_sb[cc][:, cols], in_=c_dram[cc * P : (cc + 1) * P, cols])
         load_b(1)
         x_sb = keep.tile([P, PACK, PIXELS], BF16, name="x_sb")
         nc.sync.dma_start(out=x_sb[:], in_=x_dram.rearrange("(t p) j -> p t j", p=P))
@@ -113,13 +116,20 @@ def tile_dualattention_pa_kernel(tc, c_feat, b_feat, x, w3, b3, alpha, out):
                 in_=grouped[:, cols, :].rearrange("p col t -> p (col t)"),
             )
 
+        def warm_up():
+            zeros = keep.tile([P, BANK], BF16, name="zeros")
+            nc.vector.memset(zeros[:], 0.0)
+            unread = psum.tile([P, BANK], F32, name="unread", tag="bank")
+            for repeat in range(WARM_UP):
+                nc.tensor.matmul(out=unread[:], lhsT=zeros[:, 0:P], rhs=zeros[:], start=True, stop=True)
+
         score_banks = {}
         exps = {}
 
         def scores(jt):
             score_banks[jt] = [psum.tile([P, BANK], F32, name="score_bank", tag="bank") for h in range(HALVES)]
-            for cc in range(C_CHUNKS):
-                for h in range(HALVES):
+            for h in range(HALVES):
+                for cc in range(C_CHUNKS):
                     nc.tensor.matmul(
                         out=score_banks[jt][h][:],
                         lhsT=b_sb[jt // 2][:, cc, tile_of(jt % 2)],
@@ -251,6 +261,7 @@ def tile_dualattention_pa_kernel(tc, c_feat, b_feat, x, w3, b3, alpha, out):
 
         all_channels = slice(0, CHANNELS)
 
+        warm_up()
         scores(0)
         bank_maxima(0)
         negated_maximum(0)

@@ -103,10 +103,20 @@ def tile_dualattention_pa_kernel(tc, c_feat, b_feat, x, w3, b3, alpha, out):
         def tile_of(index):
             return slice(index * P, (index + 1) * P)
 
-        def regroup(engine_copy, grouped, rows, cols):
+        def regroup(engine_copy, grouped, rows):
             engine_copy(
-                out=grouped[:, cols, :].rearrange("p (c i) t -> p c t i", i=RUN),
-                in_=rows[:, :, cols].rearrange("p t (c i) -> p c t i", i=RUN),
+                out=grouped.rearrange("p (c i) t -> p c t i", i=RUN),
+                in_=rows.rearrange("p t (c i) -> p c t i", i=RUN),
+            )
+
+        def regroup_on_gpsimd(grouped, rows):
+            nc.gpsimd.tensor_scalar(
+                out=grouped,
+                in0=rows.rearrange("p t c -> p c t"),
+                scalar1=1.0,
+                scalar2=0.0,
+                op0=ALU.mult,
+                op1=ALU.add,
             )
 
         def quantise(codes, scales, grouped, cols):
@@ -118,7 +128,7 @@ def tile_dualattention_pa_kernel(tc, c_feat, b_feat, x, w3, b3, alpha, out):
 
         def warm_up():
             zeros = keep.tile([P, BANK], BF16, name="zeros")
-            nc.vector.memset(zeros[:], 0.0)
+            nc.vector.memset(zeros[:].bitcast(U32), 0)
             unread = psum.tile([P, BANK], F32, name="unread", tag="bank")
             for repeat in range(WARM_UP):
                 nc.tensor.matmul(out=unread[:], lhsT=zeros[:, 0:P], rhs=zeros[:], start=True, stop=True)
@@ -126,22 +136,21 @@ def tile_dualattention_pa_kernel(tc, c_feat, b_feat, x, w3, b3, alpha, out):
         score_banks = {}
         exps = {}
 
-        def scores(jt):
-            score_banks[jt] = [psum.tile([P, BANK], F32, name="score_bank", tag="bank") for h in range(HALVES)]
-            for h in range(HALVES):
-                for cc in range(C_CHUNKS):
-                    nc.tensor.matmul(
-                        out=score_banks[jt][h][:],
-                        lhsT=b_sb[jt // 2][:, cc, tile_of(jt % 2)],
-                        rhs=c_sb[cc][:, half(h)],
-                        start=(cc == 0),
-                        stop=(cc == C_CHUNKS - 1),
-                    )
+        def scores(jt, h):
+            score_banks[(jt, h)] = psum.tile([P, BANK], F32, name="score_bank", tag="bank")
+            for cc in range(C_CHUNKS):
+                nc.tensor.matmul(
+                    out=score_banks[(jt, h)][:],
+                    lhsT=b_sb[jt // 2][:, cc, tile_of(jt % 2)],
+                    rhs=c_sb[cc][:, half(h)],
+                    start=(cc == 0),
+                    stop=(cc == C_CHUNKS - 1),
+                )
 
         def bank_maxima(jt):
             for h in range(HALVES):
                 nc.vector.tensor_reduce(
-                    out=bank_max[:, jt, h : h + 1], in_=score_banks[jt][h][:], axis=AX.X, op=ALU.max
+                    out=bank_max[:, jt, h : h + 1], in_=score_banks[(jt, h)][:], axis=AX.X, op=ALU.max
                 )
 
         def negated_maximum(jt):
@@ -154,7 +163,7 @@ def tile_dualattention_pa_kernel(tc, c_feat, b_feat, x, w3, b3, alpha, out):
             for h in range(HALVES):
                 nc.scalar.activation(
                     out=exps[jt][:, half(h)],
-                    in_=score_banks[jt][h][:],
+                    in_=score_banks[(jt, h)][:],
                     func=ACT.Exp,
                     bias=neg_max[:, jt : jt + 1],
                     scale=1.0,
@@ -180,14 +189,21 @@ def tile_dualattention_pa_kernel(tc, c_feat, b_feat, x, w3, b3, alpha, out):
                 op1=ALU.add,
             )
 
-        def transpose_w3():
+        w_banks = {}
+
+        def transpose_w3_on_tensor():
             for oh in range(2):
-                wt = psum.tile([P, PACK, 2 * P], BF16, name="wt", tag="bank")
+                w_banks[oh] = psum.tile([P, PACK, 2 * P], BF16, name="w_bank", tag="bank")
                 for t in range(PACK):
                     for o2 in range(2):
-                        nc.tensor.transpose(wt[:, t, tile_of(o2)], w_sb[:, 2 * oh + o2, tile_of(t)], identity[:])
+                        nc.tensor.transpose(
+                            w_banks[oh][:, t, tile_of(o2)], w_sb[:, 2 * oh + o2, tile_of(t)], identity[:]
+                        )
+
+        def copy_w3_on_scalar():
+            for oh in range(2):
                 nc.scalar.copy(
-                    out=w_grouped[:, oh * 2 * P : (oh + 1) * 2 * P, :], in_=wt[:].rearrange("p t o -> p o t")
+                    out=w_grouped[:, oh * 2 * P : (oh + 1) * 2 * P, :], in_=w_banks[oh][:].rearrange("p t o -> p o t")
                 )
 
         d_banks = {}
@@ -262,43 +278,49 @@ def tile_dualattention_pa_kernel(tc, c_feat, b_feat, x, w3, b3, alpha, out):
         all_channels = slice(0, CHANNELS)
 
         warm_up()
-        scores(0)
+        scores(0, 0)
+        scores(0, 1)
         bank_maxima(0)
         negated_maximum(0)
         exponentials(0)
         sum_of(0)
 
-        scores(1)
+        scores(1, 0)
+        scores(1, 1)
         bank_maxima(1)
-        regroup(nc.vector.tensor_copy, x_grouped, x_sb, half(0))
+        regroup(nc.vector.tensor_copy, x_grouped[:, half(0), :], x_sb[:, :, half(0)])
         negated_maximum(1)
         exponentials(1)
         sum_of(1)
         reciprocal_of(0)
         normalise(0)
 
-        scores(2)
-        transpose_w3()
+        scores(2, 0)
+        scores(2, 1)
+        scores(3, 0)
+        transpose_w3_on_tensor()
         bank_maxima(2)
-        regroup(nc.vector.tensor_copy, x_grouped, x_sb, half(1))
+        regroup(nc.vector.tensor_copy, x_grouped[:, half(1), :], x_sb[:, :, half(1)])
         negated_maximum(2)
+        copy_w3_on_scalar()
         exponentials(2)
         sum_of(2)
-        reciprocal_of(1)
-        normalise(1)
 
-        scores(3)
+        scores(3, 1)
         bank_maxima(3)
         quantise(x_codes, x_scales, x_grouped, half(0))
+        reciprocal_of(1)
+        normalise(1)
         negated_maximum(3)
         exponentials(3)
         sum_of(3)
         quantise(x_codes, x_scales, x_grouped, half(1))
+
+        scores(4, 0)
+        scores(4, 1)
+        bank_maxima(4)
         reciprocal_of(2)
         normalise(2)
-
-        scores(4)
-        bank_maxima(4)
         quantise(w_codes, w_scales, w_grouped, all_channels)
         negated_maximum(4)
         exponentials(4)
@@ -307,37 +329,40 @@ def tile_dualattention_pa_kernel(tc, c_feat, b_feat, x, w3, b3, alpha, out):
         reciprocal_of(3)
         normalise(3)
 
-        scores(5)
+        scores(5, 0)
+        scores(5, 1)
         project(0)
         bank_maxima(5)
         add_bias(0, 0)
         negated_maximum(5)
         exponentials(5)
+        regroup(nc.scalar.copy, a_grouped[0][:, quarter(0), :], a_rows[0][:, :, quarter(0)])
         sum_of(5)
-        regroup(nc.scalar.copy, a_grouped[0], a_rows[0], quarter(0))
+        regroup(nc.scalar.copy, a_grouped[0][:, quarter(1), :], a_rows[0][:, :, quarter(1)])
         add_bias(0, 1)
         add_bias(0, 2)
         add_bias(0, 3)
-        regroup(nc.scalar.copy, a_grouped[0], a_rows[0], quarter(1))
         reciprocal_of(4)
         normalise(4)
 
-        scores(6)
+        scores(6, 0)
+        scores(6, 1)
         project(1)
         bank_maxima(6)
         add_bias(1, 0)
         negated_maximum(6)
         exponentials(6)
+        regroup(nc.scalar.copy, a_grouped[0][:, quarter(2), :], a_rows[0][:, :, quarter(2)])
         sum_of(6)
-        regroup(nc.scalar.copy, a_grouped[0], a_rows[0], quarter(2))
-        add_bias(1, 1)
+        regroup(nc.scalar.copy, a_grouped[0][:, quarter(3), :], a_rows[0][:, :, quarter(3)])
         quantise(d_codes[0], d_scales[0], d_grouped[0], all_channels)
         quantise(a_codes[0], a_scales[0], a_grouped[0], half(0))
-        regroup(nc.scalar.copy, a_grouped[0], a_rows[0], quarter(3))
+        add_bias(1, 1)
         reciprocal_of(5)
         normalise(5)
 
-        scores(7)
+        scores(7, 0)
+        scores(7, 1)
         attend(0, 0)
         bank_maxima(7)
         reciprocal_of(6)
@@ -348,13 +373,13 @@ def tile_dualattention_pa_kernel(tc, c_feat, b_feat, x, w3, b3, alpha, out):
         add_bias(1, 2)
         add_bias(1, 3)
         quantise(d_codes[1], d_scales[1], d_grouped[1], all_channels)
-        quantise(a_codes[0], a_scales[0], a_grouped[0], half(1))
-        attend(0, 1)
 
         reciprocal_of(7)
+        quantise(a_codes[0], a_scales[0], a_grouped[0], half(1))
+        attend(0, 1)
         normalise_on_vector(7)
-        regroup(nc.scalar.copy, a_grouped[1], a_rows[1], half(1))
-        regroup(nc.vector.tensor_copy, a_grouped[1], a_rows[1], half(0))
+        regroup(nc.scalar.copy, a_grouped[1][:, half(1), :], a_rows[1][:, :, half(1)])
+        regroup(nc.vector.tensor_copy, a_grouped[1][:, half(0), :], a_rows[1][:, :, half(0)])
         quantise(a_codes[1], a_scales[1], a_grouped[1], half(0))
         attend(1, 0)
         quantise(a_codes[1], a_scales[1], a_grouped[1], half(1))

@@ -208,8 +208,8 @@ def tile_dualattention_pa_kernel(tc, c_feat, b_feat, x, w3, b3, alpha, out):
 
         d_banks = {}
 
-        def project(g):
-            for oc in range(C_CHUNKS):
+        def project(g, chunks=range(C_CHUNKS)):
+            for oc in chunks:
                 d_banks[(g, oc)] = psum.tile([P, PACK, P], F32, name="d_bank", tag="bank")
                 for t in range(PACK):
                     nc.tensor.matmul_mx(
@@ -279,13 +279,13 @@ def tile_dualattention_pa_kernel(tc, c_feat, b_feat, x, w3, b3, alpha, out):
 
         warm_up()
         scores(0, 0)
+        scores(1, 0)
         scores(0, 1)
         bank_maxima(0)
         negated_maximum(0)
         exponentials(0)
         sum_of(0)
 
-        scores(1, 0)
         scores(1, 1)
         bank_maxima(1)
         regroup(nc.vector.tensor_copy, x_grouped[:, half(0), :], x_sb[:, :, half(0)])
@@ -331,57 +331,57 @@ def tile_dualattention_pa_kernel(tc, c_feat, b_feat, x, w3, b3, alpha, out):
 
         scores(5, 0)
         scores(5, 1)
-        project(0)
         bank_maxima(5)
-        add_bias(0, 0)
         negated_maximum(5)
         exponentials(5)
-        regroup(nc.scalar.copy, a_grouped[0][:, quarter(0), :], a_rows[0][:, :, quarter(0)])
         sum_of(5)
-        regroup(nc.scalar.copy, a_grouped[0][:, quarter(1), :], a_rows[0][:, :, quarter(1)])
-        add_bias(0, 1)
-        add_bias(0, 2)
-        add_bias(0, 3)
-        reciprocal_of(4)
-        normalise(4)
 
         scores(6, 0)
         scores(6, 1)
-        project(1)
+        project(0)
         bank_maxima(6)
-        add_bias(1, 0)
+        reciprocal_of(4)
+        normalise(4)
+        add_bias(0, 0)
         negated_maximum(6)
         exponentials(6)
-        regroup(nc.scalar.copy, a_grouped[0][:, quarter(2), :], a_rows[0][:, :, quarter(2)])
         sum_of(6)
-        regroup(nc.scalar.copy, a_grouped[0][:, quarter(3), :], a_rows[0][:, :, quarter(3)])
-        quantise(d_codes[0], d_scales[0], d_grouped[0], all_channels)
-        quantise(a_codes[0], a_scales[0], a_grouped[0], half(0))
-        add_bias(1, 1)
+        regroup(nc.scalar.copy, a_grouped[0][:, quarter(0), :], a_rows[0][:, :, quarter(0)])
+        add_bias(0, 1)
+        add_bias(0, 2)
         reciprocal_of(5)
         normalise(5)
 
         scores(7, 0)
         scores(7, 1)
-        attend(0, 0)
+        project(1)
         bank_maxima(7)
-        reciprocal_of(6)
-        normalise(6)
+        add_bias(0, 3)
         negated_maximum(7)
         exponentials(7)
         sum_of(7)
+        regroup(nc.scalar.copy, a_grouped[0][:, quarter(1), :], a_rows[0][:, :, quarter(1)])
+        regroup(nc.scalar.copy, a_grouped[0][:, quarter(2), :], a_rows[0][:, :, quarter(2)])
+        regroup(nc.scalar.copy, a_grouped[0][:, quarter(3), :], a_rows[0][:, :, quarter(3)])
+        reciprocal_of(6)
+        normalise(6)
+        add_bias(1, 0)
+        add_bias(1, 1)
         add_bias(1, 2)
         add_bias(1, 3)
-        quantise(d_codes[1], d_scales[1], d_grouped[1], all_channels)
 
         reciprocal_of(7)
-        quantise(a_codes[0], a_scales[0], a_grouped[0], half(1))
-        attend(0, 1)
+        quantise(d_codes[0], d_scales[0], d_grouped[0], all_channels)
         normalise_on_vector(7)
         regroup(nc.scalar.copy, a_grouped[1][:, half(1), :], a_rows[1][:, :, half(1)])
+        quantise(a_codes[0], a_scales[0], a_grouped[0], half(0))
+        attend(0, 0)
         regroup(nc.vector.tensor_copy, a_grouped[1][:, half(0), :], a_rows[1][:, :, half(0)])
+        quantise(d_codes[1], d_scales[1], d_grouped[1], all_channels)
         quantise(a_codes[1], a_scales[1], a_grouped[1], half(0))
         attend(1, 0)
+        quantise(a_codes[0], a_scales[0], a_grouped[0], half(1))
+        attend(0, 1)
         quantise(a_codes[1], a_scales[1], a_grouped[1], half(1))
         attend(1, 1)
         scale_on_scalar(0, 1)

from contextlib import ExitStack

import concourse.mybir as mybir
from concourse.masks import make_identity

BF16 = mybir.dt.bfloat16
F32 = mybir.dt.float32
U32 = mybir.dt.uint32
U8 = mybir.dt.uint8
FP8X4 = mybir.dt.float8_e4m3fn_x4
ALU = mybir.AluOpType
ACT = mybir.ActivationFunctionType
AX = mybir.AxisListType

P = 128
PACK = 4
CHANNELS = 512
PIXELS = 1024
BANK = 512
C_CHUNKS = CHANNELS // P
J_PASSES = PIXELS // (P * PACK)
HALVES = PIXELS // BANK
B_QUARTERS = 4
WARM_UP = 4
RUN = 4

FLOPS = 2 * CHANNELS * CHANNELS * PIXELS + 2 * 2 * PIXELS * PIXELS * CHANNELS


def tile_dualattention_pa_kernel(tc, c_feat, b_feat, x, w3, b3, alpha, out):
    nc = tc.nc
    c_dram = c_feat.rearrange("b c n -> (b c) n")
    b_dram = b_feat.rearrange("b c n -> (b c) n")
    x_dram = x.rearrange("b c h w -> (b c) (h w)")
    out_dram = out.rearrange("b c h w -> (b c) (h w)")

    with ExitStack() as pools:
        keep = pools.enter_context(tc.tile_pool(name="keep", bufs=1))
        exp_pool = pools.enter_context(tc.tile_pool(name="exp", bufs=4))
        res_pool = pools.enter_context(tc.tile_pool(name="res", bufs=8))
        psum = pools.enter_context(tc.psum_pool(name="psum", bufs=8))
        pools.enter_context(tc.manual_schedule())

        b_view = b_dram.rearrange("(cc p) j -> p cc j", p=P)
        b_sb = [keep.tile([P, C_CHUNKS, 2 * P], BF16, name="b_sb%d" % q) for q in range(B_QUARTERS)]
        c_sb = [keep.tile([P, PIXELS], BF16, name="c_sb%d" % cc) for cc in range(C_CHUNKS)]

        def load_b(q):
            nc.sync.dma_start(out=b_sb[q][:], in_=b_view[:, :, q * 2 * P : (q + 1) * 2 * P])

        load_b(0)
        for h in range(HALVES):
            for cc in range(C_CHUNKS):
                cols = slice(h * BANK, (h + 1) * BANK)
                nc.sync.dma_start(out=c_sb[cc][:, cols], in_=c_dram[cc * P : (cc + 1) * P, cols])
        load_b(1)
        x_sb = keep.tile([P, PACK, PIXELS], BF16, name="x_sb")
        nc.sync.dma_start(out=x_sb[:], in_=x_dram.rearrange("(t p) j -> p t j", p=P))
        w_sb = keep.tile([P, C_CHUNKS, CHANNELS], BF16, name="w_sb")
        nc.sync.dma_start(out=w_sb[:], in_=w3.rearrange("(ot p) c -> p ot c", p=P))
        load_b(2)
        load_b(3)
        bias_sb = keep.tile([P, CHANNELS], BF16, name="bias_sb")
        nc.sync.dma_start(out=bias_sb[:], in_=b3.partition_broadcast(P))
        alpha_bf = keep.tile([P, 1], BF16, name="alpha_bf")
        nc.sync.dma_start(out=alpha_bf[:], in_=alpha.partition_broadcast(P))
        alpha_f32 = keep.tile([P, 1], F32, name="alpha_f32")

        identity = keep.tile([P, P], BF16, name="identity")
        make_identity(nc, identity[:])

        x_grouped = keep.tile([P, PIXELS, PACK], BF16, name="x_grouped", align_bytes=64)
        x_codes = keep.tile([P, PIXELS], U32, name="x_codes", align_bytes=64)
        x_scales = keep.tile([P, PIXELS], U8, name="x_scales", align_bytes=64)
        w_grouped = keep.tile([P, CHANNELS, PACK], BF16, name="w_grouped", align_bytes=64)
        w_codes = keep.tile([P, CHANNELS], U32, name="w_codes", align_bytes=64)
        w_scales = keep.tile([P, CHANNELS], U8, name="w_scales", align_bytes=64)
        d_grouped = [
            keep.tile([P, CHANNELS, PACK], BF16, name="d_grouped%d" % g, align_bytes=64) for g in range(J_PASSES)
        ]
        d_codes = [keep.tile([P, CHANNELS], U32, name="d_codes%d" % g, align_bytes=64) for g in range(J_PASSES)]
        d_scales = [keep.tile([P, CHANNELS], U8, name="d_scales%d" % g, align_bytes=64) for g in range(J_PASSES)]
        a_rows = [keep.tile([P, PACK, PIXELS], BF16, name="a_rows%d" % g) for g in range(J_PASSES)]
        a_grouped = [
            keep.tile([P, PIXELS, PACK], BF16, name="a_grouped%d" % g, align_bytes=64) for g in range(J_PASSES)
        ]
        a_codes = [keep.tile([P, PIXELS], U32, name="a_codes%d" % g, align_bytes=64) for g in range(J_PASSES)]
        a_scales = [keep.tile([P, PIXELS], U8, name="a_scales%d" % g, align_bytes=64) for g in range(J_PASSES)]
        j_tiles = J_PASSES * PACK
        bank_max = keep.tile([P, j_tiles, HALVES], F32, name="bank_max")
        neg_max = keep.tile([P, j_tiles], F32, name="neg_max")
        bank_sum = keep.tile([P, j_tiles, HALVES], F32, name="bank_sum")
        sum_copy = keep.tile([P, j_tiles, HALVES], F32, name="sum_copy")
        total = keep.tile([P, j_tiles], F32, name="total")
        inv_total = keep.tile([P, j_tiles], F32, name="inv_total")

        def half(h):
            return slice(h * BANK, (h + 1) * BANK)

        def quarter(q):
            return slice(q * BANK // 2, (q + 1) * BANK // 2)

        def tile_of(index):
            return slice(index * P, (index + 1) * P)

        def regroup(engine_copy, grouped, rows):
            engine_copy(
                out=grouped.rearrange("p (c i) t -> p c t i", i=RUN),
                in_=rows.rearrange("p t (c i) -> p c t i", i=RUN),
            )

        def regroup_on_gpsimd(grouped, rows):
            nc.gpsimd.tensor_scalar(
                out=grouped,
                in0=rows.rearrange("p t c -> p c t"),
                scalar1=1.0,
                scalar2=0.0,
                op0=ALU.mult,
                op1=ALU.add,
            )

        def quantise(codes, scales, grouped, cols):
            nc.vector.quantize_mx(
                out=codes[:, cols].bitcast(FP8X4),
                scales=scales[:, cols],
                in_=grouped[:, cols, :].rearrange("p col t -> p (col t)"),
            )

        def warm_up():
            zeros = keep.tile([P, BANK], BF16, name="zeros")
            nc.vector.memset(zeros[:].bitcast(U32), 0)
            unread = psum.tile([P, BANK], F32, name="unread", tag="bank")
            for repeat in range(WARM_UP):
                nc.tensor.matmul(out=unread[:], lhsT=zeros[:, 0:P], rhs=zeros[:], start=True, stop=True)

        score_banks = {}
        exps = {}

        def scores(jt, h):
            score_banks[(jt, h)] = psum.tile([P, BANK], F32, name="score_bank", tag="bank")
            for cc in range(C_CHUNKS):
                nc.tensor.matmul(
                    out=score_banks[(jt, h)][:],
                    lhsT=b_sb[jt // 2][:, cc, tile_of(jt % 2)],
                    rhs=c_sb[cc][:, half(h)],
                    start=(cc == 0),
                    stop=(cc == C_CHUNKS - 1),
                )

        def bank_maxima(jt):
            for h in range(HALVES):
                nc.vector.tensor_reduce(
                    out=bank_max[:, jt, h : h + 1], in_=score_banks[(jt, h)][:], axis=AX.X, op=ALU.max
                )

        def negated_maximum(jt):
            nc.vector.tensor_reduce(
                out=neg_max[:, jt : jt + 1], in_=bank_max[:, jt, :], axis=AX.X, op=ALU.max, negate=True
            )

        def exponentials(jt):
            exps[jt] = exp_pool.tile([P, PIXELS], F32, name="e")
            for h in range(HALVES):
                nc.scalar.activation(
                    out=exps[jt][:, half(h)],
                    in_=score_banks[(jt, h)][:],
                    func=ACT.Exp,
                    bias=neg_max[:, jt : jt + 1],
                    scale=1.0,
                    accum_out=bank_sum[:, jt, h : h + 1],
                )

        def sum_of(jt):
            nc.scalar.activation(
                out=sum_copy[:, jt, :], in_=bank_sum[:, jt, :], func=ACT.Copy, accum_out=total[:, jt : jt + 1]
            )

        def reciprocal_of(jt):
            nc.vector.reciprocal(out=inv_total[:, jt : jt + 1], in_=total[:, jt : jt + 1])

        def normalise(jt):
            g, t = divmod(jt, PACK)
            nc.gpsimd.tensor_scalar(
                out=a_rows[g][:, t, :],
                in0=exps[jt][:],
                scalar1=inv_total[:, jt : jt + 1],
                scalar2=0.0,
                op0=ALU.mult,
                op1=ALU.add,
            )

        w_banks = {}

        def transpose_w3_on_tensor():
            for oh in range(2):
                w_banks[oh] = psum.tile([P, PACK, 2 * P], BF16, name="w_bank", tag="bank")
                for t in range(PACK):
                    for o2 in range(2):
                        nc.tensor.transpose(
                            w_banks[oh][:, t, tile_of(o2)], w_sb[:, 2 * oh + o2, tile_of(t)], identity[:]
                        )

        def copy_w3_on_scalar():
            for oh in range(2):
                nc.scalar.copy(
                    out=w_grouped[:, oh * 2 * P : (oh + 1) * 2 * P, :], in_=w_banks[oh][:].rearrange("p t o -> p o t")
                )

        d_banks = {}

        def project(g, chunks=range(C_CHUNKS)):
            for oc in chunks:
                d_banks[(g, oc)] = psum.tile([P, PACK, P], F32, name="d_bank", tag="bank")
                for t in range(PACK):
                    nc.tensor.matmul_mx(
                        out=d_banks[(g, oc)][:, t, :],
                        lhsT=x_codes[:, tile_of(g * PACK + t)].bitcast(FP8X4),
                        lhsT_scale=x_scales[:, tile_of(g * PACK + t)],
                        rhs=w_codes[:, tile_of(oc)].bitcast(FP8X4),
                        rhs_scale=w_scales[:, tile_of(oc)],
                        start=True,
                        stop=True,
                    )

        def add_bias(g, oc):
            nc.vector.tensor_tensor(
                out=d_grouped[g][:, tile_of(oc), :],
                in0=d_banks[(g, oc)][:].rearrange("p t o -> p o t"),
                in1=bias_sb[:, tile_of(oc)].unsqueeze(2).to_broadcast([P, P, PACK]),
                op=ALU.add,
            )

        acc = {}

        def attend(g, h):
            for ct in range(C_CHUNKS):
                if g == 0:
                    acc[(h, ct)] = psum.tile([P, BANK], F32, name="acc", tag="bank")
                nc.tensor.matmul_mx(
                    out=acc[(h, ct)][:],
                    lhsT=d_codes[g][:, tile_of(ct)].bitcast(FP8X4),
                    lhsT_scale=d_scales[g][:, tile_of(ct)],
                    rhs=a_codes[g][:, half(h)].bitcast(FP8X4),
                    rhs_scale=a_scales[g][:, half(h)],
                    start=(g == 0),
                    stop=(g == J_PASSES - 1),
                )

        def finish(h, ct):
            res = res_pool.tile([P, BANK], F32, name="res")
            nc.vector.scalar_tensor_tensor(
                out=res[:],
                in0=acc[(h, ct)][:],
                scalar=alpha_f32[:, 0:1],
                in1=x_sb[:, ct, half(h)],
                op0=ALU.mult,
                op1=ALU.add,
            )
            nc.sync.dma_start(out=out_dram[tile_of(ct), half(h)], in_=res[:])

        def normalise_on_vector(jt):
            g, t = divmod(jt, PACK)
            nc.vector.tensor_scalar(
                out=a_rows[g][:, t, :], in0=exps[jt][:], scalar1=inv_total[:, jt : jt + 1], scalar2=None, op0=ALU.mult
            )

        scaled = {}

        def scale_on_scalar(h, ct):
            scaled[(h, ct)] = res_pool.tile([P, BANK], F32, name="scaled")
            nc.scalar.activation(out=scaled[(h, ct)][:], in_=acc[(h, ct)][:], func=ACT.Copy, scale=alpha_f32[:, 0:1])

        def add_x_on_gpsimd(h, ct):
            res = res_pool.tile([P, BANK], F32, name="res")
            nc.gpsimd.tensor_tensor(out=res[:], in0=scaled[(h, ct)][:], in1=x_sb[:, ct, half(h)], op=ALU.add)
            nc.sync.dma_start(out=out_dram[tile_of(ct), half(h)], in_=res[:])

        all_channels = slice(0, CHANNELS)

        warm_up()
        scores(0, 0)
        scores(1, 0)
        scores(0, 1)
        bank_maxima(0)
        negated_maximum(0)
        exponentials(0)
        sum_of(0)

        scores(1, 1)
        bank_maxima(1)
        regroup(nc.vector.tensor_copy, x_grouped[:, half(0), :], x_sb[:, :, half(0)])
        negated_maximum(1)
        exponentials(1)
        sum_of(1)
        reciprocal_of(0)
        normalise(0)

        scores(2, 0)
        scores(2, 1)
        scores(3, 0)
        transpose_w3_on_tensor()
        bank_maxima(2)
        regroup(nc.vector.tensor_copy, x_grouped[:, half(1), :], x_sb[:, :, half(1)])
        negated_maximum(2)
        copy_w3_on_scalar()
        exponentials(2)
        sum_of(2)

        scores(3, 1)
        bank_maxima(3)
        quantise(x_codes, x_scales, x_grouped, half(0))
        reciprocal_of(1)
        normalise(1)
        negated_maximum(3)
        exponentials(3)
        sum_of(3)
        quantise(x_codes, x_scales, x_grouped, half(1))

        scores(4, 0)
        scores(4, 1)
        bank_maxima(4)
        reciprocal_of(2)
        normalise(2)
        quantise(w_codes, w_scales, w_grouped, all_channels)
        negated_maximum(4)
        exponentials(4)
        sum_of(4)
        nc.vector.tensor_copy(out=alpha_f32[:], in_=alpha_bf[:])
        reciprocal_of(3)
        normalise(3)

        scores(5, 0)
        scores(5, 1)
        bank_maxima(5)
        negated_maximum(5)
        exponentials(5)
        sum_of(5)

        scores(6, 0)
        scores(6, 1)
        project(0)
        bank_maxima(6)
        reciprocal_of(4)
        normalise(4)
        add_bias(0, 0)
        negated_maximum(6)
        exponentials(6)
        sum_of(6)
        regroup(nc.scalar.copy, a_grouped[0][:, quarter(0), :], a_rows[0][:, :, quarter(0)])
        add_bias(0, 1)
        add_bias(0, 2)
        reciprocal_of(5)
        normalise(5)

        scores(7, 0)
        scores(7, 1)
        project(1)
        bank_maxima(7)
        add_bias(0, 3)
        negated_maximum(7)
        exponentials(7)
        sum_of(7)
        regroup(nc.scalar.copy, a_grouped[0][:, quarter(1), :], a_rows[0][:, :, quarter(1)])
        regroup(nc.scalar.copy, a_grouped[0][:, quarter(2), :], a_rows[0][:, :, quarter(2)])
        regroup(nc.scalar.copy, a_grouped[0][:, quarter(3), :], a_rows[0][:, :, quarter(3)])
        reciprocal_of(6)
        normalise(6)
        add_bias(1, 0)
        add_bias(1, 1)
        add_bias(1, 2)
        add_bias(1, 3)

        reciprocal_of(7)
        quantise(d_codes[0], d_scales[0], d_grouped[0], all_channels)
        normalise_on_vector(7)
        regroup(nc.scalar.copy, a_grouped[1][:, half(1), :], a_rows[1][:, :, half(1)])
        quantise(a_codes[0], a_scales[0], a_grouped[0], half(0))
        attend(0, 0)
        regroup(nc.vector.tensor_copy, a_grouped[1][:, half(0), :], a_rows[1][:, :, half(0)])
        quantise(d_codes[1], d_scales[1], d_grouped[1], all_channels)
        quantise(a_codes[1], a_scales[1], a_grouped[1], half(0))
        attend(1, 0)
        quantise(a_codes[0], a_scales[0], a_grouped[0], half(1))
        attend(0, 1)
        quantise(a_codes[1], a_scales[1], a_grouped[1], half(1))
        attend(1, 1)
        scale_on_scalar(0, 1)
        scale_on_scalar(0, 3)
        finish(0, 0)
        finish(0, 2)
        add_x_on_gpsimd(0, 1)
        finish(1, 0)
        finish(1, 1)
        add_x_on_gpsimd(0, 3)
        finish(1, 2)
        finish(1, 3)
